import numpy as np
import ml_dtypes


def mxq(x, axis, fmt="e4m3"):
    dtype, down = {"e4m3": (ml_dtypes.float8_e4m3fn, 7), "e5m2": (ml_dtypes.float8_e5m2, 14)}[fmt]
    v = np.moveaxis(np.asarray(x, np.float32).astype(ml_dtypes.bfloat16).astype(np.float64), axis, -1)
    blocks = v.reshape(v.shape[:-1] + (-1, 32))
    amax = np.abs(blocks).max(-1, keepdims=True)
    byte = np.maximum(np.where(amax > 0, np.frexp(amax)[1] - 1 + 127, 0) - down, 1)
    scale = np.exp2(byte - 127.0)
    codes = (blocks / scale).astype(np.float32).astype(dtype).astype(np.float64)
    return np.moveaxis((codes * scale).reshape(v.shape), -1, axis)


WIDE = False


def mx_kscale(k):
    if not WIDE:
        return np.ones(k)
    levels = np.array([10, -10, 5, -5, 0])
    if k % 512:
        return np.exp2(np.random.permutation(np.resize(levels, k // 32))).repeat(32)
    a = np.empty((k // 512, 16))
    for p in range(k // 512):
        a[p, :8] = np.random.permutation(np.resize(levels, 8))
        for g in range(8):
            far = levels[np.abs(levels - a[p, g]) >= 10]
            a[p, g + 8] = far[np.random.randint(len(far))]
    return np.exp2(a.ravel()).repeat(32)


BF16 = ml_dtypes.bfloat16


def bf(x):
    return np.asarray(x, np.float32).astype(BF16)


def f64(x):
    return np.asarray(x).astype(np.float64)


B, N, C, F = 4, 32, 1024, 1024
EPS_STD = 1e-5


def setup_inputs():
    u, s = mx_kscale(C), mx_kscale(C)
    rows = np.concatenate([u, u, s])
    return {"x": bf(np.random.standard_normal((B, N, C)) * u),
            "e_enc": bf(np.random.standard_normal((B, N, N, C)) * s),
            "W_pre": bf(np.random.standard_normal((3 * C, F)) / np.sqrt(3 * C) / rows[:, None]),
            "b_pre": bf(np.random.standard_normal(F) * 0.3)}


def core(x, e_enc, W_pre, b_pre):
    w = f64(W_pre)
    xq = mxq(f64(x), 2, "e4m3")
    tgt = xq @ mxq(w[:C], 0, "e4m3")
    src = xq @ mxq(w[C:2 * C], 0, "e4m3")
    edg = mxq(f64(e_enc), 3, "e4m3") @ mxq(w[2 * C:], 0, "e4m3")
    m = tgt[:, :, None, :] + src[:, None, :, :] + edg + f64(b_pre)
    mean = m.mean(axis=2)
    mn = m.min(axis=2)
    mx = m.max(axis=2)
    var = (m * m).mean(axis=2) - mean * mean
    std = np.sqrt(np.maximum(var, 0.0) + EPS_STD)
    return np.concatenate([mean, mn, mx, std], axis=-1)


def e4m3fn_bytes(y):
    return np.clip(np.asarray(y, np.float64), -448.0, 448.0).astype(np.float32).astype(ml_dtypes.float8_e4m3fn).view(np.uint8)


def reference(x, e_enc, W_pre, b_pre):
    out = core(x, e_enc, W_pre, b_pre)
    s = np.max(np.abs(out), axis=-1, keepdims=True) / 448.0
    return out, e4m3fn_bytes(out / s)

@@ -1,0 +1,433 @@
+from contextlib import ExitStack
+
+import concourse.mybir as mybir
+from concourse.masks import make_identity
+
+F32 = mybir.dt.float32
+BF16 = mybir.dt.bfloat16
+I32 = mybir.dt.int32
+U8 = mybir.dt.uint8
+FP8X4 = mybir.dt.float8_e4m3fn_x4
+FP8 = mybir.dt.float8_e4m3fn
+ALU = mybir.AluOpType
+ACT = mybir.ActivationFunctionType
+AX = mybir.AxisListType
+
+P = 128
+NSRC = 32
+TGT_BLK = 16
+NBLK = 8
+NFT = 8
+FLOPS = 2 * 4096 * 1024 * 1024 + 2 * 2 * 128 * 1024 * 1024
+
+W_ENGINE = "vvssssss"
+SQ_ON_VECTOR = ((7, 4), (7, 5), (7, 6), (7, 7))
+FIN_ON_VECTOR = (6, 7)
+S_FTS = (1, 6)
+PE_FTS = (0, 2, 4)
+
+
+def tile_gnnlayer_pa_kernel(tc, x, e_enc, W_pre, b_pre, out_0, out_1):
+    nc = tc.nc
+    x_flat = x.flatten_outer_dims()
+    e_flat = e_enc.flatten_outer_dims()
+    out0_v = out_0.flatten_outer_dims().rearrange("r (a c) -> r a c", a=4)
+    out1_flat = out_1.flatten_outer_dims()
+
+    with ExitStack() as ctx:
+        const = ctx.enter_context(tc.tile_pool(name="const", bufs=1))
+        keep = ctx.enter_context(tc.tile_pool(name="keep", bufs=1))
+        stream = ctx.enter_context(tc.tile_pool(name="stream", bufs=2))
+        psum_a = ctx.enter_context(tc.psum_pool(name="psum_a", bufs=4))
+        psum_t = ctx.enter_context(tc.psum_pool(name="psum_t", bufs=2))
+        psum_q = ctx.enter_context(tc.psum_pool(name="psum_q", bufs=2))
+
+        ident = const.tile([P, P], F32, name="ident")
+        make_identity(nc, ident[:])
+        eps_t = const.tile([P, 1], F32, name="eps_t")
+        nc.vector.memset(eps_t[:], 1e-5)
+        zero_t = const.tile([P, 1], F32, name="zero_t")
+        nc.vector.memset(zero_t[:], 0.0)
+        junk = const.tile([P, 1], F32, name="junk")
+        nc.scalar.activation(out=junk[:], in_=eps_t[:], func=ACT.Sqrt)
+
+        wc = keep.tile([P, NFT, 512], I32, name="wc", align_bytes=64)
+        ws = keep.tile([P, NFT, 512], U8, name="ws", align_bytes=64)
+        w1c = keep.tile([P, 2, 1024], I32, name="w1c", align_bytes=64)
+        w1s = keep.tile([P, 2, 1024], U8, name="w1s", align_bytes=64)
+        xc = keep.tile([P, 256], I32, name="xc", align_bytes=64)
+        xs = keep.tile([P, 256], U8, name="xs", align_bytes=64)
+        xr = keep.tile([P, 4, 1024], I32, name="xr", align_bytes=64)
+        xrs = keep.tile([P, 4, 1024], U8, name="xrs", align_bytes=64)
+        res = keep.tile([P, NFT, 4, P], F32, name="res")
+        sm = keep.tile([P, NFT, P], F32, name="sm")
+        sq = keep.tile([P, NFT, P], F32, name="sq")
+        tb = keep.tile([P, NFT, P], F32, name="tb")
+        out_sb = keep.tile([P, 4, 1024], F32, name="out_sb")
+        f8 = keep.tile([P, 4096], FP8, name="f8")
+        pm = keep.tile([P, 16], F32, name="pm")
+        bb = keep.tile([P, NFT], BF16, name="bb")
+        bcol = keep.tile([P, NFT], F32, name="bcol")
+        ssum = keep.tile([P, 16], F32, name="ssum")
+        ssum32 = keep.tile([P, 16], F32, name="ssum32")
+
+        er_tiles = {}
+
+        def e_load(blk):
+            er = stream.tile([P, 4, 1024], BF16, name="er", tag="er", bufs=3)
+            if blk == 0:
+                for t in range(4):
+                    nc.sync.dma_start(out=er[:, t, :], in_=e_flat[P * t : P * (t + 1), :])
+            else:
+                nc.sync.dma_start(
+                    out=er[:],
+                    in_=e_flat[512 * blk : 512 * (blk + 1), :].rearrange("(t p) k -> p t k", p=P),
+                )
+            er_tiles[blk] = er
+
+        def w_load(rows_cols, pieces=1):
+            wr = stream.tile([P, 4, 4, 512], BF16, name="wr", tag="wr", bufs=2)
+            width = 512 // pieces
+            for piece in range(pieces):
+                for s, (r0, c0) in enumerate(rows_cols):
+                    lo = piece * width
+                    nc.sync.dma_start(
+                        out=wr[:, s, :, lo : lo + width],
+                        in_=W_pre[r0 : r0 + 512, c0 + lo : c0 + lo + width].rearrange("(p j) w -> p j w", j=4),
+                    )
+            return wr
+
+        x_sb = keep.tile([P, 1024], BF16, name="x_sb")
+        nc.sync.dma_start(out=x_sb[:], in_=x_flat)
+        e_load(0)
+        wr23 = [None, None]
+        wr23[0] = w_load([(2048, 0), (2560, 0), (1024, 0), (1536, 0)], pieces=2)
+        wr23[1] = w_load([(2048, 512), (2560, 512), (1024, 512), (1536, 512)], pieces=2)
+        e_load(1)
+        e_load(2)
+        with nc.allow_non_contiguous_dma(reason="the bias, one element to a partition"):
+            nc.sync.dma_start(out=bb[:], in_=b_pre.rearrange("(t p) -> p t", p=P))
+
+        x_w = x_sb[:].bitcast(F32)
+        x_t = psum_t.tile([P, 4, P], F32, name="x_t", tag="xt")
+        for g in range(2):
+            for u in range(2):
+                nc.tensor.transpose(
+                    out=x_t[:, 2 * g + u, :], in_=x_w[:, 256 * g + u : 256 * (g + 1) : 2], identity=ident[:]
+                )
+        xg = keep.tile([P, 1024], BF16, name="xg", align_bytes=64)
+        nc.scalar.copy(
+            out=xg[:].bitcast(F32).rearrange("p (g r u) -> p g r u", g=2, u=2),
+            in_=x_t[:].rearrange("p (g u) r -> p g r u", u=2),
+        )
+        nc.vector.quantize_mx(out=xc[:].bitcast(FP8X4), scales=xs[:], in_=xg[:])
+
+        def x_repeat(b, on_vector):
+            xgr = stream.tile([P, 4096], BF16, name="xgr", tag="gr", bufs=3, align_bytes=64)
+            for g in range(2):
+                interleave(
+                    on_vector,
+                    xgr[:].bitcast(F32).rearrange("p (g j i u) -> p g j i u", g=2, j=NSRC, u=2)[:, g, :, :, :],
+                    xg[:]
+                    .bitcast(F32)
+                    .rearrange("p (g r u) -> p g r u", g=2, u=2)[:, g, NSRC * b : NSRC * (b + 1), :]
+                    .unsqueeze(2)
+                    .to_broadcast([P, NSRC, TGT_BLK, 2]),
+                )
+            nc.vector.quantize_mx(out=xr[:, b, :].bitcast(FP8X4), scales=xrs[:, b, :], in_=xgr[:])
+
+        gr_tiles = {}
+        ec_tiles = {}
+
+        def e_transpose(blk, g, tp):
+            er = er_tiles[blk]
+            if g == 0 and tp == 0:
+                gr_new = stream.tile([P, 4096], BF16, name="gr", tag="gr", bufs=3, align_bytes=64)
+                gr_tiles[blk] = gr_new
+            gr = gr_tiles[blk]
+            xt = psum_t.tile([P, 2, 2, P], F32, name="xt", tag="xt")
+            for tt in range(2):
+                e_w = er[:, 2 * tp + tt, :].bitcast(F32)
+                for u in range(2):
+                    nc.tensor.transpose(
+                        out=xt[:, u, tt, :], in_=e_w[:, 256 * g + u : 256 * (g + 1) : 2], identity=ident[:]
+                    )
+            nc.scalar.copy(
+                out=gr[:].bitcast(F32).rearrange("p (g j i u) -> p g j i u", g=2, j=NSRC, u=2)[
+                    :, g, :, 8 * tp : 8 * (tp + 1), :
+                ],
+                in_=xt[:].rearrange("p u tt (il j) -> p j (tt il) u", j=NSRC),
+            )
+
+        def e_quant(blk):
+            ec = stream.tile([P, 2, 512], I32, name="ec", tag="ec", bufs=2, align_bytes=64)
+            es = stream.tile([P, 2, 512], U8, name="es", tag="es", bufs=2, align_bytes=64)
+            ec_tiles[blk] = (ec, es)
+            nc.vector.quantize_mx(
+                out=ec[:].rearrange("p g c -> p (g c)").bitcast(FP8X4),
+                scales=es[:].rearrange("p g c -> p (g c)"),
+                in_=gr_tiles[blk][:],
+            )
+
+        def interleave(who, dst, src):
+            if who == "v":
+                nc.vector.tensor_copy(out=dst, in_=src)
+            elif who == "g":
+                nc.gpsimd.tensor_scalar(out=dst, in0=src, scalar1=1.0, scalar2=0.0, op0=ALU.mult, op1=ALU.add)
+            else:
+                nc.scalar.copy(out=dst, in_=src)
+
+        def w_prep(ft):
+            wr = wr23[ft // 4]
+            c0 = (ft % 4) * P
+            wg = stream.tile([P, 2048], BF16, name="wg", tag="wg", bufs=4, align_bytes=64)
+            interleave(
+                W_ENGINE[ft],
+                wg[:].rearrange("p (s f j) -> p s f j", s=4, j=4),
+                wr[:, :, :, c0 : c0 + P].rearrange("p s j f -> p s f j"),
+            )
+            nc.vector.quantize_mx(out=wc[:, ft, :].bitcast(FP8X4), scales=ws[:, ft, :], in_=wg[:])
+
+        w1r_box = []
+
+        def w1_load():
+            w1r_box.append(w_load([(0, 0), (0, 512), (512, 0), (512, 512)]))
+
+        def w1_prep(g, h):
+            wg = stream.tile([P, 2048], BF16, name="wg", tag="wg", bufs=4, align_bytes=64)
+            interleave(
+                "s",
+                wg[:].rearrange("p (f j) -> p f j", j=4),
+                w1r_box[0][:, 2 * g + h, :, :].rearrange("p j f -> p f j"),
+            )
+            nc.vector.quantize_mx(
+                out=w1c[:, g, 512 * h : 512 * (h + 1)].bitcast(FP8X4),
+                scales=w1s[:, g, 512 * h : 512 * (h + 1)],
+                in_=wg[:],
+            )
+
+        def target_term(half):
+            if half == 0:
+                nc.vector.tensor_copy(out=bcol[:], in_=bb[:])
+            tp = psum_t.tile([P, 4, P], F32, name="tp", tag="xt")
+            for q in range(4):
+                ft = 4 * half + q
+                for g in range(2):
+                    nc.tensor.matmul_mx(
+                        out=tp[:, q, :],
+                        lhsT=w1c[:, g, P * ft : P * (ft + 1)].bitcast(FP8X4),
+                        lhsT_scale=w1s[:, g, P * ft : P * (ft + 1)],
+                        rhs=xc[:, P * g : P * (g + 1)].bitcast(FP8X4),
+                        rhs_scale=xs[:, P * g : P * (g + 1)],
+                        start=(g == 0),
+                        stop=(g == 1),
+                    )
+            for q in range(4):
+                ft = 4 * half + q
+                nc.scalar.activation(
+                    out=tb[:, ft, :], in_=tp[:, q, :], func=ACT.Identity, bias=bcol[:, ft : ft + 1], scale=1.0
+                )
+
+        def source_sums():
+            st = psum_t.tile([P, 4, P], F32, name="st", tag="xt")
+            for q, ft in enumerate(PE_FTS):
+                for g in range(2):
+                    nc.tensor.matmul_mx(
+                        out=st[:, q, :],
+                        lhsT=wc[:, ft, P * (2 + g) : P * (3 + g)].bitcast(FP8X4),
+                        lhsT_scale=ws[:, ft, P * (2 + g) : P * (3 + g)],
+                        rhs=xc[:, P * g : P * (g + 1)].bitcast(FP8X4),
+                        rhs_scale=xs[:, P * g : P * (g + 1)],
+                        start=(g == 0),
+                        stop=(g == 1),
+                    )
+            nc.vector.tensor_reduce(
+                out=ssum[:, 0:12].rearrange("p (q b) -> p q b", b=4),
+                in_=st[:, 0:3, :].rearrange("p q (b j) -> p q b j", j=NSRC),
+                axis=AX.X,
+                op=ALU.add,
+            )
+            nc.vector.tensor_scalar(
+                out=ssum32[:, 0:12], in0=ssum[:, 0:12], scalar1=1.0 / NSRC, scalar2=None, op0=ALU.mult
+            )
+
+        pq_box = {}
+        sqt_box = {}
+
+        def bank(blk, ft):
+            b = blk // 2
+            ec, es = ec_tiles[blk]
+            acc = psum_a.tile([P, 512], F32, name="acc", tag="acc")
+            operands = (
+                (2, xr[:, b, 0:512], xrs[:, b, 0:512]),
+                (3, xr[:, b, 512:1024], xrs[:, b, 512:1024]),
+                (0, ec[:, 0, :], es[:, 0, :]),
+                (1, ec[:, 1, :], es[:, 1, :]),
+            )
+            for n, (s, rhs, rhs_scale) in enumerate(operands):
+                nc.tensor.matmul_mx(
+                    out=acc[:],
+                    lhsT=wc[:, ft, P * s : P * (s + 1)].bitcast(FP8X4),
+                    lhsT_scale=ws[:, ft, P * s : P * (s + 1)],
+                    rhs=rhs.bitcast(FP8X4),
+                    rhs_scale=rhs_scale,
+                    start=(n == 0),
+                    stop=(n == 3),
+                )
+            cols = slice(TGT_BLK * blk, TGT_BLK * (blk + 1))
+            if ft in PE_FTS:
+                if ft == 0:
+                    pq_new = psum_q.tile([P, 4, P], F32, name="pq", tag="pq")
+                    pq_box[0] = pq_new
+                pq = pq_box[0]
+                for g in range(2):
+                    for jh in range(4):
+                        nc.tensor.matmul_mx(
+                            out=pq[:, ft // 2, :],
+                            lhsT=wc[:, ft, P * g : P * (g + 1)].bitcast(FP8X4),
+                            lhsT_scale=ws[:, ft, P * g : P * (g + 1)],
+                            rhs=ec[:, g, P * jh : P * (jh + 1)].bitcast(FP8X4),
+                            rhs_scale=es[:, g, P * jh : P * (jh + 1)],
+                            start=(g == 0 and jh == 0),
+                            stop=(g == 1 and jh == 3),
+                        )
+            acc_v = acc[:].rearrange("p (j i) -> p i j", i=TGT_BLK)
+            if ft % 4 == 0:
+                sqt_new = stream.tile([P, 4, NSRC, TGT_BLK], F32, name="sqt", tag="sqt", bufs=3)
+                sqt_box[0] = sqt_new
+            sqt = sqt_box[0]
+            nc.vector.tensor_reduce(out=res[:, ft, 2, cols], in_=acc_v, axis=AX.X, op=ALU.max)
+            nc.vector.tensor_reduce(out=res[:, ft, 1, cols], in_=acc_v, axis=AX.X, op=ALU.min)
+            on_scalar = ft in S_FTS and blk < NBLK - 1
+            if ft not in PE_FTS and not on_scalar:
+                nc.vector.tensor_reduce(out=sm[:, ft, cols], in_=acc_v, axis=AX.X, op=ALU.add)
+            nc.scalar.activation(
+                out=sqt[:, ft % 4, :, :], in_=acc[:].rearrange("p (j i) -> p j i", i=TGT_BLK), func=ACT.Square
+            )
+            if on_scalar:
+                for i in range(TGT_BLK):
+                    junk_row = stream.tile([P, NSRC], F32, name="junk_row", tag="junk_row", bufs=2)
+                    nc.scalar.activation(
+                        out=junk_row[:],
+                        in_=acc_v[:, i, :],
+                        func=ACT.Copy,
+                        accum_out=sm[:, ft, TGT_BLK * blk + i : TGT_BLK * blk + i + 1],
+                    )
+            if ft == PE_FTS[2]:
+                nc.vector.tensor_reduce(
+                    out=sm[:, 0:6:2, cols],
+                    in_=pq_box[0][:, 0:3, :].rearrange("p q (j i) -> p q i j", i=TGT_BLK),
+                    axis=AX.X,
+                    op=ALU.add,
+                )
+            if (blk, ft) in SQ_ON_VECTOR:
+                nc.vector.tensor_reduce(
+                    out=sq[:, ft, cols], in_=sqt[:, ft % 4, :, :].rearrange("p j i -> p i j"), axis=AX.X, op=ALU.add
+                )
+            elif ft % 4 == 3:
+                w = NSRC // 2
+                while w > 1:
+                    nc.gpsimd.tensor_tensor(
+                        out=sqt[:, :, 0:w, :], in0=sqt[:, :, 0:w, :], in1=sqt[:, :, w : 2 * w, :], op=ALU.add
+                    )
+                    w = w // 2
+                nc.gpsimd.tensor_tensor(
+                    out=sq[:, ft - 3 : ft + 1, cols], in0=sqt[:, :, 0, :], in1=sqt[:, :, 1, :], op=ALU.add
+                )
+
+        def finish(ft):
+            eng = nc.vector if ft in FIN_ON_VECTOR else nc.gpsimd
+            if ft in PE_FTS:
+                for b in range(4):
+                    nc.scalar.activation(
+                        out=res[:, ft, 0, NSRC * b : NSRC * (b + 1)],
+                        in_=sm[:, ft, NSRC * b : NSRC * (b + 1)],
+                        func=ACT.Identity,
+                        bias=ssum32[:, 4 * (ft // 2) + b : 4 * (ft // 2) + b + 1],
+                        scale=1.0 / NSRC,
+                    )
+            else:
+                nc.scalar.activation(out=res[:, ft, 0, :], in_=sm[:, ft, :], func=ACT.Copy, scale=1.0 / NSRC)
+            m2 = stream.tile([P, P], F32, name="m2", tag="m2", bufs=2)
+            nc.scalar.activation(out=m2[:], in_=res[:, ft, 0, :], func=ACT.Square, scale=NSRC**0.5)
+            dv = stream.tile([P, P], F32, name="dv", tag="dv", bufs=2)
+            eng.tensor_tensor(out=dv[:], in0=sq[:, ft, :], in1=m2[:], op=ALU.subtract)
+            dr = stream.tile([P, P], F32, name="dr", tag="dr", bufs=2)
+            nc.scalar.activation(out=dr[:], in_=dv[:], func=ACT.Relu, scale=1.0 / NSRC)
+            nc.scalar.activation(out=res[:, ft, 3, :], in_=dr[:], func=ACT.Sqrt, bias=eps_t[:, 0:1], scale=1.0)
+            eng.tensor_tensor(
+                out=res[:, ft, 0:3, :],
+                in0=res[:, ft, 0:3, :],
+                in1=tb[:, ft, :].unsqueeze(1).to_broadcast([P, 3, P]),
+                op=ALU.add,
+            )
+            tr = psum_t.tile([P, 4, P], F32, name="tr", tag="xt")
+            for a in range(4):
+                nc.tensor.transpose(out=tr[:, a, :], in_=res[:, ft, a, :], identity=ident[:])
+            fcols = slice(P * ft, P * (ft + 1))
+            nc.scalar.copy(out=out_sb[:, :, fcols], in_=tr[:])
+            nc.vector.tensor_reduce(out=pm[:, ft : ft + 1], in_=tr[:, 2:4, :], axis=AX.XY, op=ALU.max)
+            nc.vector.tensor_reduce(out=pm[:, 8 + ft : 9 + ft], in_=tr[:, 1, :], axis=AX.X, op=ALU.min)
+            nc.sync.dma_start(out=out0_v[:, :, fcols], in_=out_sb[:, :, fcols])
+
+        x_repeat(0, "v")
+        for g in range(2):
+            for tp in range(2):
+                e_transpose(0, g, tp)
+        e_quant(0)
+        for ft in range(4):
+            w_prep(ft)
+
+        for blk in range(NBLK):
+            for ft in range(NFT):
+                if blk == 0 and ft + 4 < NFT:
+                    w_prep(ft + 4)
+                bank(blk, ft)
+                if blk + 1 < NBLK:
+                    if ft in (0, 2):
+                        e_transpose(blk + 1, ft // 2, 0)
+                        e_transpose(blk + 1, ft // 2, 1)
+                    if ft == 4:
+                        e_quant(blk + 1)
+                if ft == 3 and blk % 2 == 1 and blk < 7:
+                    x_repeat((blk + 1) // 2, "s")
+                if ft == 6 and blk + 3 < NBLK:
+                    e_load(blk + 3)
+                if blk == 0 and ft == 7:
+                    w1_load()
+                if blk == 1 and ft == 5:
+                    source_sums()
+                if blk == 3 and ft >= 4:
+                    w1_prep((ft - 4) // 2, (ft - 4) % 2)
+                if blk == 4 and ft in (3, 7):
+                    target_term(0 if ft == 3 else 1)
+                if blk == NBLK - 1:
+                    if ft == 5:
+                        finish(1)
+                        finish(3)
+                    if ft == 6:
+                        finish(0)
+                        finish(2)
+                    if ft == 7:
+                        for late in range(4, NFT):
+                            finish(late)
+
+        amax = const.tile([P, 1], F32, name="amax")
+        nc.vector.tensor_reduce(out=amax[:], in_=pm[:], axis=AX.X, op=ALU.max, apply_absolute_value=True)
+        rcp = const.tile([P, 1], F32, name="rcp")
+        nc.vector.reciprocal(out=rcp[:], in_=amax[:])
+        fac = const.tile([P, 1], F32, name="fac")
+        nc.vector.tensor_scalar(out=fac[:], in0=rcp[:], scalar1=448.0, scalar2=None, op0=ALU.mult)
+        out_all = out_sb[:].rearrange("p a c -> p (a c)")
+        for on_vector, c0, c1 in ((True, 0, 1408), (False, 2752, 3424), (True, 1408, 2752), (False, 3424, 4096)):
+            if on_vector:
+                nc.vector.tensor_scalar(
+                    out=f8[:, c0:c1], in0=out_all[:, c0:c1], scalar1=fac[:, 0:1], scalar2=None, op0=ALU.mult,
+                    saturate=False,
+                )
+            else:
+                nc.scalar.activation(
+                    out=f8[:, c0:c1], in_=out_all[:, c0:c1], func=ACT.Identity, scale=fac[:, 0:1],
+                    bias=zero_t[:, 0:1], saturate=False,
+                )
+            nc.sync.dma_start(out=out1_flat[:, c0:c1], in_=f8[:, c0:c1].bitcast(U8))

@@ -38,9 +38,9 @@ def tile_gnnlayer_pa_kernel(tc, x, e_enc, W_pre, b_pre, out_0, out_1):
         const = ctx.enter_context(tc.tile_pool(name="const", bufs=1))
         keep = ctx.enter_context(tc.tile_pool(name="keep", bufs=1))
         stream = ctx.enter_context(tc.tile_pool(name="stream", bufs=2))
-        psum_a = ctx.enter_context(tc.psum_pool(name="psum_a", bufs=4))
+        psum_a = ctx.enter_context(tc.psum_pool(name="psum_a", bufs=5))
         psum_t = ctx.enter_context(tc.psum_pool(name="psum_t", bufs=2))
-        psum_q = ctx.enter_context(tc.psum_pool(name="psum_q", bufs=2))
+        psum_q = ctx.enter_context(tc.psum_pool(name="psum_q", bufs=1))
 
         ident = const.tile([P, P], F32, name="ident")
         make_identity(nc, ident[:])

@@ -122,6 +122,8 @@ def tile_gnnlayer_pa_kernel(tc, x, e_enc, W_pre, b_pre, out_0, out_1):
         )
         nc.vector.quantize_mx(out=xc[:].bitcast(FP8X4), scales=xs[:], in_=xg[:])
 
+        xgr_box = {}
+
         def x_repeat(b, on_vector):
             xgr = stream.tile([P, 4096], BF16, name="xgr", tag="gr", bufs=3, align_bytes=64)
             for g in range(2):
@@ -134,7 +136,10 @@ def tile_gnnlayer_pa_kernel(tc, x, e_enc, W_pre, b_pre, out_0, out_1):
                     .unsqueeze(2)
                     .to_broadcast([P, NSRC, TGT_BLK, 2]),
                 )
-            nc.vector.quantize_mx(out=xr[:, b, :].bitcast(FP8X4), scales=xrs[:, b, :], in_=xgr[:])
+            xgr_box[b] = xgr
+
+        def x_quant(b):
+            nc.vector.quantize_mx(out=xr[:, b, :].bitcast(FP8X4), scales=xrs[:, b, :], in_=xgr_box[b][:])
 
         gr_tiles = {}
         ec_tiles = {}
@@ -189,6 +194,7 @@ def tile_gnnlayer_pa_kernel(tc, x, e_enc, W_pre, b_pre, out_0, out_1):
             nc.vector.quantize_mx(out=wc[:, ft, :].bitcast(FP8X4), scales=ws[:, ft, :], in_=wg[:])
 
         w1r_box = []
+        w1g_box = {}
 
         def w1_load():
             w1r_box.append(w_load([(0, 0), (0, 512), (512, 0), (512, 512)]))
@@ -200,10 +206,13 @@ def tile_gnnlayer_pa_kernel(tc, x, e_enc, W_pre, b_pre, out_0, out_1):
                 wg[:].rearrange("p (f j) -> p f j", j=4),
                 w1r_box[0][:, 2 * g + h, :, :].rearrange("p j f -> p f j"),
             )
+            w1g_box[(g, h)] = wg
+
+        def w1_quant(g, h):
             nc.vector.quantize_mx(
                 out=w1c[:, g, 512 * h : 512 * (h + 1)].bitcast(FP8X4),
                 scales=w1s[:, g, 512 * h : 512 * (h + 1)],
-                in_=wg[:],
+                in_=w1g_box[(g, h)][:],
             )
 
         def target_term(half):
@@ -254,6 +263,18 @@ def tile_gnnlayer_pa_kernel(tc, x, e_enc, W_pre, b_pre, out_0, out_1):
         pq_box = {}
         sqt_box = {}
 
+        def quantise_in_the_gap(blk, ft):
+            if ft == 3 and blk + 1 < NBLK:
+                e_quant(blk + 1)
+            if ft == 3 and blk % 2 == 1 and blk < 7:
+                x_quant((blk + 1) // 2)
+            if (blk, ft) == (3, 7):
+                w1_quant(0, 0)
+                w1_quant(1, 0)
+            if (blk, ft) == (4, 3):
+                w1_quant(0, 1)
+                w1_quant(1, 1)
+
         def bank(blk, ft):
             b = blk // 2
             ec, es = ec_tiles[blk]
@@ -301,6 +322,8 @@ def tile_gnnlayer_pa_kernel(tc, x, e_enc, W_pre, b_pre, out_0, out_1):
             on_scalar = ft in S_FTS and blk < NBLK - 1
             if ft not in PE_FTS and not on_scalar:
                 nc.vector.tensor_reduce(out=sm[:, ft, cols], in_=acc_v, axis=AX.X, op=ALU.add)
+            if ft % 4 == 3:
+                quantise_in_the_gap(blk, ft)
             nc.scalar.activation(
                 out=sqt[:, ft % 4, :, :], in_=acc[:].rearrange("p (j i) -> p j i", i=TGT_BLK), func=ACT.Square
             )
@@ -355,15 +378,15 @@ def tile_gnnlayer_pa_kernel(tc, x, e_enc, W_pre, b_pre, out_0, out_1):
             dr = stream.tile([P, P], F32, name="dr", tag="dr", bufs=2)
             nc.scalar.activation(out=dr[:], in_=dv[:], func=ACT.Relu, scale=1.0 / NSRC)
             nc.scalar.activation(out=res[:, ft, 3, :], in_=dr[:], func=ACT.Sqrt, bias=eps_t[:, 0:1], scale=1.0)
-            eng.tensor_tensor(
-                out=res[:, ft, 0:3, :],
-                in0=res[:, ft, 0:3, :],
-                in1=tb[:, ft, :].unsqueeze(1).to_broadcast([P, 3, P]),
-                op=ALU.add,
-            )
             tr = psum_t.tile([P, 4, P], F32, name="tr", tag="xt")
-            for a in range(4):
-                nc.tensor.transpose(out=tr[:, a, :], in_=res[:, ft, a, :], identity=ident[:])
+            for a in range(3):
+                nc.tensor.matmul(
+                    out=tr[:, a, :], lhsT=res[:, ft, a, :], rhs=ident[:], is_transpose=True, start=True, stop=False
+                )
+                nc.tensor.matmul(
+                    out=tr[:, a, :], lhsT=tb[:, ft, :], rhs=ident[:], is_transpose=True, start=False, stop=True
+                )
+            nc.tensor.transpose(out=tr[:, 3, :], in_=res[:, ft, 3, :], identity=ident[:])
             fcols = slice(P * ft, P * (ft + 1))
             nc.scalar.copy(out=out_sb[:, :, fcols], in_=tr[:])
             nc.vector.tensor_reduce(out=pm[:, ft : ft + 1], in_=tr[:, 2:4, :], axis=AX.XY, op=ALU.max)
@@ -371,6 +394,7 @@ def tile_gnnlayer_pa_kernel(tc, x, e_enc, W_pre, b_pre, out_0, out_1):
             nc.sync.dma_start(out=out0_v[:, :, fcols], in_=out_sb[:, :, fcols])
 
         x_repeat(0, "v")
+        x_quant(0)
         for g in range(2):
             for tp in range(2):
                 e_transpose(0, g, tp)
@@ -387,9 +411,7 @@ def tile_gnnlayer_pa_kernel(tc, x, e_enc, W_pre, b_pre, out_0, out_1):
                     if ft in (0, 2):
                         e_transpose(blk + 1, ft // 2, 0)
                         e_transpose(blk + 1, ft // 2, 1)
-                    if ft == 4:
-                        e_quant(blk + 1)
-                if ft == 3 and blk % 2 == 1 and blk < 7:
+                if ft == 0 and blk % 2 == 1 and blk < 7:
                     x_repeat((blk + 1) // 2, "s")
                 if ft == 6 and blk + 3 < NBLK:
                     e_load(blk + 3)
@@ -397,10 +419,10 @@ def tile_gnnlayer_pa_kernel(tc, x, e_enc, W_pre, b_pre, out_0, out_1):
                     w1_load()
                 if blk == 1 and ft == 5:
                     source_sums()
-                if blk == 3 and ft >= 4:
-                    w1_prep((ft - 4) // 2, (ft - 4) % 2)
-                if blk == 4 and ft in (3, 7):
-                    target_term(0 if ft == 3 else 1)
+                if blk == 3 and ft < 4:
+                    w1_prep(ft % 2, ft // 2)
+                if blk == 4 and ft in (5, 7):
+                    target_term(0 if ft == 5 else 1)
                 if blk == NBLK - 1:
                     if ft == 5:
                         finish(1)

@@ -23,7 +23,7 @@ FLOPS = 2 * 4096 * 1024 * 1024 + 2 * 2 * 128 * 1024 * 1024
 W_ENGINE = "vvssssss"
 SQ_ON_VECTOR = ((7, 4), (7, 5), (7, 6), (7, 7))
 FIN_ON_VECTOR = (6, 7)
-S_FTS = (1, 6)
+S_FTS = (5, 7)
 PE_FTS = (0, 2, 4)
 
 

@@ -186,11 +186,12 @@ def tile_gnnlayer_pa_kernel(tc, x, e_enc, W_pre, b_pre, out_0, out_1):
             wr = wr23[ft // 4]
             c0 = (ft % 4) * P
             wg = stream.tile([P, 2048], BF16, name="wg", tag="wg", bufs=4, align_bytes=64)
-            interleave(
-                W_ENGINE[ft],
-                wg[:].rearrange("p (s f j) -> p s f j", s=4, j=4),
-                wr[:, :, :, c0 : c0 + P].rearrange("p s j f -> p s f j"),
-            )
+            for s in range(4):
+                interleave(
+                    W_ENGINE[ft],
+                    wg[:].rearrange("p (s c i j) -> p s c j i", s=4, i=4, j=4)[:, s, :, :, :],
+                    wr[:, s, :, c0 : c0 + P].rearrange("p j (c i) -> p c j i", i=4),
+                )
             nc.vector.quantize_mx(out=wc[:, ft, :].bitcast(FP8X4), scales=ws[:, ft, :], in_=wg[:])
 
         w1r_box = []
@@ -203,8 +204,8 @@ def tile_gnnlayer_pa_kernel(tc, x, e_enc, W_pre, b_pre, out_0, out_1):
             wg = stream.tile([P, 2048], BF16, name="wg", tag="wg", bufs=4, align_bytes=64)
             interleave(
                 "s",
-                wg[:].rearrange("p (f j) -> p f j", j=4),
-                w1r_box[0][:, 2 * g + h, :, :].rearrange("p j f -> p f j"),
+                wg[:].rearrange("p (c i j) -> p c j i", i=4, j=4),
+                w1r_box[0][:, 2 * g + h, :, :].rearrange("p j (c i) -> p c j i", i=4),
             )
             w1g_box[(g, h)] = wg
 

@@ -264,6 +264,30 @@ def tile_gnnlayer_pa_kernel(tc, x, e_enc, W_pre, b_pre, out_0, out_1):
         pq_box = {}
         sqt_box = {}
 
+        tree_box = []
+
+        def tree_level(tree, level):
+            tile, ft, cols = tree
+            w = NSRC >> level
+            if w > 1:
+                nc.gpsimd.tensor_tensor(
+                    out=tile[:, :, 0:w, :], in0=tile[:, :, 0:w, :], in1=tile[:, :, w : 2 * w, :], op=ALU.add
+                )
+            else:
+                nc.gpsimd.tensor_tensor(
+                    out=sq[:, ft - 3 : ft + 1, cols], in0=tile[:, :, 0, :], in1=tile[:, :, 1, :], op=ALU.add
+                )
+
+        def tree_step(new):
+            old = tree_box.pop() if tree_box else None
+            for old_level, new_level in ((3, 1), (4, 2), (5, None)):
+                if old is not None:
+                    tree_level(old, old_level)
+                if new is not None and new_level is not None:
+                    tree_level(new, new_level)
+            if new is not None:
+                tree_box.append(new)
+
         def quantise_in_the_gap(blk, ft):
             if ft == 3 and blk + 1 < NBLK:
                 e_quant(blk + 1)
@@ -349,15 +373,9 @@ def tile_gnnlayer_pa_kernel(tc, x, e_enc, W_pre, b_pre, out_0, out_1):
                     out=sq[:, ft, cols], in_=sqt[:, ft % 4, :, :].rearrange("p j i -> p i j"), axis=AX.X, op=ALU.add
                 )
             elif ft % 4 == 3:
-                w = NSRC // 2
-                while w > 1:
-                    nc.gpsimd.tensor_tensor(
-                        out=sqt[:, :, 0:w, :], in0=sqt[:, :, 0:w, :], in1=sqt[:, :, w : 2 * w, :], op=ALU.add
-                    )
-                    w = w // 2
-                nc.gpsimd.tensor_tensor(
-                    out=sq[:, ft - 3 : ft + 1, cols], in0=sqt[:, :, 0, :], in1=sqt[:, :, 1, :], op=ALU.add
-                )
+                tree_step((sqt, ft, cols))
+                if blk == NBLK - 1:
+                    tree_step(None)
 
         def finish(ft):
             eng = nc.vector if ft in FIN_ON_VECTOR else nc.gpsimd
@@ -394,6 +412,7 @@ def tile_gnnlayer_pa_kernel(tc, x, e_enc, W_pre, b_pre, out_0, out_1):
             nc.vector.tensor_reduce(out=pm[:, 8 + ft : 9 + ft], in_=tr[:, 1, :], axis=AX.X, op=ALU.min)
             nc.sync.dma_start(out=out0_v[:, :, fcols], in_=out_sb[:, :, fcols])
 
+        ctx.enter_context(tc.manual_schedule(engines={mybir.EngineType.Pool}))
         x_repeat(0, "v")
         x_quant(0)
         for g in range(2):

from contextlib import ExitStack

import concourse.mybir as mybir
from concourse.masks import make_identity

F32 = mybir.dt.float32
BF16 = mybir.dt.bfloat16
I32 = mybir.dt.int32
U8 = mybir.dt.uint8
FP8X4 = mybir.dt.float8_e4m3fn_x4
FP8 = mybir.dt.float8_e4m3fn
ALU = mybir.AluOpType
ACT = mybir.ActivationFunctionType
AX = mybir.AxisListType

P = 128
NSRC = 32
TGT_BLK = 16
NBLK = 8
NFT = 8
FLOPS = 2 * 4096 * 1024 * 1024 + 2 * 2 * 128 * 1024 * 1024

W_ENGINE = "vvssssss"
SQ_ON_VECTOR = ((7, 4), (7, 5), (7, 6), (7, 7))
FIN_ON_VECTOR = (6, 7)
S_FTS = (5, 7)
PE_FTS = (0, 2, 4)


def tile_gnnlayer_pa_kernel(tc, x, e_enc, W_pre, b_pre, out_0, out_1):
    nc = tc.nc
    x_flat = x.flatten_outer_dims()
    e_flat = e_enc.flatten_outer_dims()
    out0_v = out_0.flatten_outer_dims().rearrange("r (a c) -> r a c", a=4)
    out1_flat = out_1.flatten_outer_dims()

    with ExitStack() as ctx:
        const = ctx.enter_context(tc.tile_pool(name="const", bufs=1))
        keep = ctx.enter_context(tc.tile_pool(name="keep", bufs=1))
        stream = ctx.enter_context(tc.tile_pool(name="stream", bufs=2))
        psum_a = ctx.enter_context(tc.psum_pool(name="psum_a", bufs=5))
        psum_t = ctx.enter_context(tc.psum_pool(name="psum_t", bufs=2))
        psum_q = ctx.enter_context(tc.psum_pool(name="psum_q", bufs=1))

        ident = const.tile([P, P], F32, name="ident")
        make_identity(nc, ident[:])
        eps_t = const.tile([P, 1], F32, name="eps_t")
        nc.vector.memset(eps_t[:], 1e-5)
        zero_t = const.tile([P, 1], F32, name="zero_t")
        nc.vector.memset(zero_t[:], 0.0)
        junk = const.tile([P, 1], F32, name="junk")
        nc.scalar.activation(out=junk[:], in_=eps_t[:], func=ACT.Sqrt)

        wc = keep.tile([P, NFT, 512], I32, name="wc", align_bytes=64)
        ws = keep.tile([P, NFT, 512], U8, name="ws", align_bytes=64)
        w1c = keep.tile([P, 2, 1024], I32, name="w1c", align_bytes=64)
        w1s = keep.tile([P, 2, 1024], U8, name="w1s", align_bytes=64)
        xc = keep.tile([P, 256], I32, name="xc", align_bytes=64)
        xs = keep.tile([P, 256], U8, name="xs", align_bytes=64)
        xr = keep.tile([P, 4, 1024], I32, name="xr", align_bytes=64)
        xrs = keep.tile([P, 4, 1024], U8, name="xrs", align_bytes=64)
        res = keep.tile([P, NFT, 4, P], F32, name="res")
        sm = keep.tile([P, NFT, P], F32, name="sm")
        sq = keep.tile([P, NFT, P], F32, name="sq")
        tb = keep.tile([P, NFT, P], F32, name="tb")
        out_sb = keep.tile([P, 4, 1024], F32, name="out_sb")
        f8 = keep.tile([P, 4096], FP8, name="f8")
        pm = keep.tile([P, 16], F32, name="pm")
        bb = keep.tile([P, NFT], BF16, name="bb")
        bcol = keep.tile([P, NFT], F32, name="bcol")
        ssum = keep.tile([P, 16], F32, name="ssum")
        ssum32 = keep.tile([P, 16], F32, name="ssum32")

        er_tiles = {}

        def e_load(blk):
            er = stream.tile([P, 4, 1024], BF16, name="er", tag="er", bufs=3)
            if blk == 0:
                for t in range(4):
                    nc.sync.dma_start(out=er[:, t, :], in_=e_flat[P * t : P * (t + 1), :])
            else:
                nc.sync.dma_start(
                    out=er[:],
                    in_=e_flat[512 * blk : 512 * (blk + 1), :].rearrange("(t p) k -> p t k", p=P),
                )
            er_tiles[blk] = er

        def w_load(rows_cols, pieces=1):
            wr = stream.tile([P, 4, 4, 512], BF16, name="wr", tag="wr", bufs=2)
            width = 512 // pieces
            for piece in range(pieces):
                for s, (r0, c0) in enumerate(rows_cols):
                    lo = piece * width
                    nc.sync.dma_start(
                        out=wr[:, s, :, lo : lo + width],
                        in_=W_pre[r0 : r0 + 512, c0 + lo : c0 + lo + width].rearrange("(p j) w -> p j w", j=4),
                    )
            return wr

        x_sb = keep.tile([P, 1024], BF16, name="x_sb")
        nc.sync.dma_start(out=x_sb[:], in_=x_flat)
        e_load(0)
        wr23 = [None, None]
        wr23[0] = w_load([(2048, 0), (2560, 0), (1024, 0), (1536, 0)], pieces=2)
        wr23[1] = w_load([(2048, 512), (2560, 512), (1024, 512), (1536, 512)], pieces=2)
        e_load(1)
        e_load(2)
        with nc.allow_non_contiguous_dma(reason="the bias, one element to a partition"):
            nc.sync.dma_start(out=bb[:], in_=b_pre.rearrange("(t p) -> p t", p=P))

        x_w = x_sb[:].bitcast(F32)
        x_t = psum_t.tile([P, 4, P], F32, name="x_t", tag="xt")
        for g in range(2):
            for u in range(2):
                nc.tensor.transpose(
                    out=x_t[:, 2 * g + u, :], in_=x_w[:, 256 * g + u : 256 * (g + 1) : 2], identity=ident[:]
                )
        xg = keep.tile([P, 1024], BF16, name="xg", align_bytes=64)
        nc.scalar.copy(
            out=xg[:].bitcast(F32).rearrange("p (g r u) -> p g r u", g=2, u=2),
            in_=x_t[:].rearrange("p (g u) r -> p g r u", u=2),
        )
        nc.vector.quantize_mx(out=xc[:].bitcast(FP8X4), scales=xs[:], in_=xg[:])

        xgr_box = {}

        def x_repeat(b, on_vector):
            xgr = stream.tile([P, 4096], BF16, name="xgr", tag="gr", bufs=3, align_bytes=64)
            for g in range(2):
                interleave(
                    on_vector,
                    xgr[:].bitcast(F32).rearrange("p (g j i u) -> p g j i u", g=2, j=NSRC, u=2)[:, g, :, :, :],
                    xg[:]
                    .bitcast(F32)
                    .rearrange("p (g r u) -> p g r u", g=2, u=2)[:, g, NSRC * b : NSRC * (b + 1), :]
                    .unsqueeze(2)
                    .to_broadcast([P, NSRC, TGT_BLK, 2]),
                )
            xgr_box[b] = xgr

        def x_quant(b):
            nc.vector.quantize_mx(out=xr[:, b, :].bitcast(FP8X4), scales=xrs[:, b, :], in_=xgr_box[b][:])

        gr_tiles = {}
        ec_tiles = {}

        def e_transpose(blk, g, tp):
            er = er_tiles[blk]
            if g == 0 and tp == 0:
                gr_new = stream.tile([P, 4096], BF16, name="gr", tag="gr", bufs=3, align_bytes=64)
                gr_tiles[blk] = gr_new
            gr = gr_tiles[blk]
            xt = psum_t.tile([P, 2, 2, P], F32, name="xt", tag="xt")
            for tt in range(2):
                e_w = er[:, 2 * tp + tt, :].bitcast(F32)
                for u in range(2):
                    nc.tensor.transpose(
                        out=xt[:, u, tt, :], in_=e_w[:, 256 * g + u : 256 * (g + 1) : 2], identity=ident[:]
                    )
            nc.scalar.copy(
                out=gr[:].bitcast(F32).rearrange("p (g j i u) -> p g j i u", g=2, j=NSRC, u=2)[
                    :, g, :, 8 * tp : 8 * (tp + 1), :
                ],
                in_=xt[:].rearrange("p u tt (il j) -> p j (tt il) u", j=NSRC),
            )

        def e_quant(blk):
            ec = stream.tile([P, 2, 512], I32, name="ec", tag="ec", bufs=2, align_bytes=64)
            es = stream.tile([P, 2, 512], U8, name="es", tag="es", bufs=2, align_bytes=64)
            ec_tiles[blk] = (ec, es)
            nc.vector.quantize_mx(
                out=ec[:].rearrange("p g c -> p (g c)").bitcast(FP8X4),
                scales=es[:].rearrange("p g c -> p (g c)"),
                in_=gr_tiles[blk][:],
            )

        def interleave(who, dst, src):
            if who == "v":
                nc.vector.tensor_copy(out=dst, in_=src)
            elif who == "g":
                nc.gpsimd.tensor_scalar(out=dst, in0=src, scalar1=1.0, scalar2=0.0, op0=ALU.mult, op1=ALU.add)
            else:
                nc.scalar.copy(out=dst, in_=src)

        def w_prep(ft):
            wr = wr23[ft // 4]
            c0 = (ft % 4) * P
            wg = stream.tile([P, 2048], BF16, name="wg", tag="wg", bufs=4, align_bytes=64)
            for s in range(4):
                interleave(
                    W_ENGINE[ft],
                    wg[:].rearrange("p (s c i j) -> p s c j i", s=4, i=4, j=4)[:, s, :, :, :],
                    wr[:, s, :, c0 : c0 + P].rearrange("p j (c i) -> p c j i", i=4),
                )
            nc.vector.quantize_mx(out=wc[:, ft, :].bitcast(FP8X4), scales=ws[:, ft, :], in_=wg[:])

        w1r_box = []
        w1g_box = {}

        def w1_load():
            w1r_box.append(w_load([(0, 0), (0, 512), (512, 0), (512, 512)]))

        def w1_prep(g, h):
            wg = stream.tile([P, 2048], BF16, name="wg", tag="wg", bufs=4, align_bytes=64)
            interleave(
                "s",
                wg[:].rearrange("p (c i j) -> p c j i", i=4, j=4),
                w1r_box[0][:, 2 * g + h, :, :].rearrange("p j (c i) -> p c j i", i=4),
            )
            w1g_box[(g, h)] = wg

        def w1_quant(g, h):
            nc.vector.quantize_mx(
                out=w1c[:, g, 512 * h : 512 * (h + 1)].bitcast(FP8X4),
                scales=w1s[:, g, 512 * h : 512 * (h + 1)],
                in_=w1g_box[(g, h)][:],
            )

        def target_term(half):
            if half == 0:
                nc.vector.tensor_copy(out=bcol[:], in_=bb[:])
            tp = psum_t.tile([P, 4, P], F32, name="tp", tag="xt")
            for q in range(4):
                ft = 4 * half + q
                for g in range(2):
                    nc.tensor.matmul_mx(
                        out=tp[:, q, :],
                        lhsT=w1c[:, g, P * ft : P * (ft + 1)].bitcast(FP8X4),
                        lhsT_scale=w1s[:, g, P * ft : P * (ft + 1)],
                        rhs=xc[:, P * g : P * (g + 1)].bitcast(FP8X4),
                        rhs_scale=xs[:, P * g : P * (g + 1)],
                        start=(g == 0),
                        stop=(g == 1),
                    )
            for q in range(4):
                ft = 4 * half + q
                nc.scalar.activation(
                    out=tb[:, ft, :], in_=tp[:, q, :], func=ACT.Identity, bias=bcol[:, ft : ft + 1], scale=1.0
                )

        def source_sums():
            st = psum_t.tile([P, 4, P], F32, name="st", tag="xt")
            for q, ft in enumerate(PE_FTS):
                for g in range(2):
                    nc.tensor.matmul_mx(
                        out=st[:, q, :],
                        lhsT=wc[:, ft, P * (2 + g) : P * (3 + g)].bitcast(FP8X4),
                        lhsT_scale=ws[:, ft, P * (2 + g) : P * (3 + g)],
                        rhs=xc[:, P * g : P * (g + 1)].bitcast(FP8X4),
                        rhs_scale=xs[:, P * g : P * (g + 1)],
                        start=(g == 0),
                        stop=(g == 1),
                    )
            nc.vector.tensor_reduce(
                out=ssum[:, 0:12].rearrange("p (q b) -> p q b", b=4),
                in_=st[:, 0:3, :].rearrange("p q (b j) -> p q b j", j=NSRC),
                axis=AX.X,
                op=ALU.add,
            )
            nc.vector.tensor_scalar(
                out=ssum32[:, 0:12], in0=ssum[:, 0:12], scalar1=1.0 / NSRC, scalar2=None, op0=ALU.mult
            )

        pq_box = {}
        sqt_box = {}

        tree_box = []

        def tree_level(tree, level):
            tile, ft, cols = tree
            w = NSRC >> level
            if w > 1:
                nc.gpsimd.tensor_tensor(
                    out=tile[:, :, 0:w, :], in0=tile[:, :, 0:w, :], in1=tile[:, :, w : 2 * w, :], op=ALU.add
                )
            else:
                nc.gpsimd.tensor_tensor(
                    out=sq[:, ft - 3 : ft + 1, cols], in0=tile[:, :, 0, :], in1=tile[:, :, 1, :], op=ALU.add
                )

        def tree_step(new):
            old = tree_box.pop() if tree_box else None
            for old_level, new_level in ((3, 1), (4, 2), (5, None)):
                if old is not None:
                    tree_level(old, old_level)
                if new is not None and new_level is not None:
                    tree_level(new, new_level)
            if new is not None:
                tree_box.append(new)

        def quantise_in_the_gap(blk, ft):
            if ft == 3 and blk + 1 < NBLK:
                e_quant(blk + 1)
            if ft == 3 and blk % 2 == 1 and blk < 7:
                x_quant((blk + 1) // 2)
            if (blk, ft) == (3, 7):
                w1_quant(0, 0)
                w1_quant(1, 0)
            if (blk, ft) == (4, 3):
                w1_quant(0, 1)
                w1_quant(1, 1)

        def bank(blk, ft):
            b = blk // 2
            ec, es = ec_tiles[blk]
            acc = psum_a.tile([P, 512], F32, name="acc", tag="acc")
            operands = (
                (2, xr[:, b, 0:512], xrs[:, b, 0:512]),
                (3, xr[:, b, 512:1024], xrs[:, b, 512:1024]),
                (0, ec[:, 0, :], es[:, 0, :]),
                (1, ec[:, 1, :], es[:, 1, :]),
            )
            for n, (s, rhs, rhs_scale) in enumerate(operands):
                nc.tensor.matmul_mx(
                    out=acc[:],
                    lhsT=wc[:, ft, P * s : P * (s + 1)].bitcast(FP8X4),
                    lhsT_scale=ws[:, ft, P * s : P * (s + 1)],
                    rhs=rhs.bitcast(FP8X4),
                    rhs_scale=rhs_scale,
                    start=(n == 0),
                    stop=(n == 3),
                )
            cols = slice(TGT_BLK * blk, TGT_BLK * (blk + 1))
            if ft in PE_FTS:
                if ft == 0:
                    pq_new = psum_q.tile([P, 4, P], F32, name="pq", tag="pq")
                    pq_box[0] = pq_new
                pq = pq_box[0]
                for g in range(2):
                    for jh in range(4):
                        nc.tensor.matmul_mx(
                            out=pq[:, ft // 2, :],
                            lhsT=wc[:, ft, P * g : P * (g + 1)].bitcast(FP8X4),
                            lhsT_scale=ws[:, ft, P * g : P * (g + 1)],
                            rhs=ec[:, g, P * jh : P * (jh + 1)].bitcast(FP8X4),
                            rhs_scale=es[:, g, P * jh : P * (jh + 1)],
                            start=(g == 0 and jh == 0),
                            stop=(g == 1 and jh == 3),
                        )
            acc_v = acc[:].rearrange("p (j i) -> p i j", i=TGT_BLK)
            if ft % 4 == 0:
                sqt_new = stream.tile([P, 4, NSRC, TGT_BLK], F32, name="sqt", tag="sqt", bufs=3)
                sqt_box[0] = sqt_new
            sqt = sqt_box[0]
            nc.vector.tensor_reduce(out=res[:, ft, 2, cols], in_=acc_v, axis=AX.X, op=ALU.max)
            nc.vector.tensor_reduce(out=res[:, ft, 1, cols], in_=acc_v, axis=AX.X, op=ALU.min)
            on_scalar = ft in S_FTS and blk < NBLK - 1
            if ft not in PE_FTS and not on_scalar:
                nc.vector.tensor_reduce(out=sm[:, ft, cols], in_=acc_v, axis=AX.X, op=ALU.add)
            if ft % 4 == 3:
                quantise_in_the_gap(blk, ft)
            nc.scalar.activation(
                out=sqt[:, ft % 4, :, :], in_=acc[:].rearrange("p (j i) -> p j i", i=TGT_BLK), func=ACT.Square
            )
            if on_scalar:
                for i in range(TGT_BLK):
                    junk_row = stream.tile([P, NSRC], F32, name="junk_row", tag="junk_row", bufs=2)
                    nc.scalar.activation(
                        out=junk_row[:],
                        in_=acc_v[:, i, :],
                        func=ACT.Copy,
                        accum_out=sm[:, ft, TGT_BLK * blk + i : TGT_BLK * blk + i + 1],
                    )
            if ft == PE_FTS[2]:
                nc.vector.tensor_reduce(
                    out=sm[:, 0:6:2, cols],
                    in_=pq_box[0][:, 0:3, :].rearrange("p q (j i) -> p q i j", i=TGT_BLK),
                    axis=AX.X,
                    op=ALU.add,
                )
            if (blk, ft) in SQ_ON_VECTOR:
                nc.vector.tensor_reduce(
                    out=sq[:, ft, cols], in_=sqt[:, ft % 4, :, :].rearrange("p j i -> p i j"), axis=AX.X, op=ALU.add
                )
            elif ft % 4 == 3:
                tree_step((sqt, ft, cols))
                if blk == NBLK - 1:
                    tree_step(None)

        def finish(ft):
            eng = nc.vector if ft in FIN_ON_VECTOR else nc.gpsimd
            if ft in PE_FTS:
                for b in range(4):
                    nc.scalar.activation(
                        out=res[:, ft, 0, NSRC * b : NSRC * (b + 1)],
                        in_=sm[:, ft, NSRC * b : NSRC * (b + 1)],
                        func=ACT.Identity,
                        bias=ssum32[:, 4 * (ft // 2) + b : 4 * (ft // 2) + b + 1],
                        scale=1.0 / NSRC,
                    )
            else:
                nc.scalar.activation(out=res[:, ft, 0, :], in_=sm[:, ft, :], func=ACT.Copy, scale=1.0 / NSRC)
            m2 = stream.tile([P, P], F32, name="m2", tag="m2", bufs=2)
            nc.scalar.activation(out=m2[:], in_=res[:, ft, 0, :], func=ACT.Square, scale=NSRC**0.5)
            dv = stream.tile([P, P], F32, name="dv", tag="dv", bufs=2)
            eng.tensor_tensor(out=dv[:], in0=sq[:, ft, :], in1=m2[:], op=ALU.subtract)
            dr = stream.tile([P, P], F32, name="dr", tag="dr", bufs=2)
            nc.scalar.activation(out=dr[:], in_=dv[:], func=ACT.Relu, scale=1.0 / NSRC)
            nc.scalar.activation(out=res[:, ft, 3, :], in_=dr[:], func=ACT.Sqrt, bias=eps_t[:, 0:1], scale=1.0)
            tr = psum_t.tile([P, 4, P], F32, name="tr", tag="xt")
            for a in range(3):
                nc.tensor.matmul(
                    out=tr[:, a, :], lhsT=res[:, ft, a, :], rhs=ident[:], is_transpose=True, start=True, stop=False
                )
                nc.tensor.matmul(
                    out=tr[:, a, :], lhsT=tb[:, ft, :], rhs=ident[:], is_transpose=True, start=False, stop=True
                )
            nc.tensor.transpose(out=tr[:, 3, :], in_=res[:, ft, 3, :], identity=ident[:])
            fcols = slice(P * ft, P * (ft + 1))
            nc.scalar.copy(out=out_sb[:, :, fcols], in_=tr[:])
            nc.vector.tensor_reduce(out=pm[:, ft : ft + 1], in_=tr[:, 2:4, :], axis=AX.XY, op=ALU.max)
            nc.vector.tensor_reduce(out=pm[:, 8 + ft : 9 + ft], in_=tr[:, 1, :], axis=AX.X, op=ALU.min)
            nc.sync.dma_start(out=out0_v[:, :, fcols], in_=out_sb[:, :, fcols])

        ctx.enter_context(tc.manual_schedule(engines={mybir.EngineType.Pool}))
        x_repeat(0, "v")
        x_quant(0)
        for g in range(2):
            for tp in range(2):
                e_transpose(0, g, tp)
        e_quant(0)
        for ft in range(4):
            w_prep(ft)

        for blk in range(NBLK):
            for ft in range(NFT):
                if blk == 0 and ft + 4 < NFT:
                    w_prep(ft + 4)
                bank(blk, ft)
                if blk + 1 < NBLK:
                    if ft in (0, 2):
                        e_transpose(blk + 1, ft // 2, 0)
                        e_transpose(blk + 1, ft // 2, 1)
                if ft == 0 and blk % 2 == 1 and blk < 7:
                    x_repeat((blk + 1) // 2, "s")
                if ft == 6 and blk + 3 < NBLK:
                    e_load(blk + 3)
                if blk == 0 and ft == 7:
                    w1_load()
                if blk == 1 and ft == 5:
                    source_sums()
                if blk == 3 and ft < 4:
                    w1_prep(ft % 2, ft // 2)
                if blk == 4 and ft in (5, 7):
                    target_term(0 if ft == 5 else 1)
                if blk == NBLK - 1:
                    if ft == 5:
                        finish(1)
                        finish(3)
                    if ft == 6:
                        finish(0)
                        finish(2)
                    if ft == 7:
                        for late in range(4, NFT):
                            finish(late)

        amax = const.tile([P, 1], F32, name="amax")
        nc.vector.tensor_reduce(out=amax[:], in_=pm[:], axis=AX.X, op=ALU.max, apply_absolute_value=True)
        rcp = const.tile([P, 1], F32, name="rcp")
        nc.vector.reciprocal(out=rcp[:], in_=amax[:])
        fac = const.tile([P, 1], F32, name="fac")
        nc.vector.tensor_scalar(out=fac[:], in0=rcp[:], scalar1=448.0, scalar2=None, op0=ALU.mult)
        out_all = out_sb[:].rearrange("p a c -> p (a c)")
        for on_vector, c0, c1 in ((True, 0, 1408), (False, 2752, 3424), (True, 1408, 2752), (False, 3424, 4096)):
            if on_vector:
                nc.vector.tensor_scalar(
                    out=f8[:, c0:c1], in0=out_all[:, c0:c1], scalar1=fac[:, 0:1], scalar2=None, op0=ALU.mult,
                    saturate=False,
                )
            else:
                nc.scalar.activation(
                    out=f8[:, c0:c1], in_=out_all[:, c0:c1], func=ACT.Identity, scale=fac[:, 0:1],
                    bias=zero_t[:, 0:1], saturate=False,
                )
            nc.sync.dma_start(out=out1_flat[:, c0:c1], in_=f8[:, c0:c1].bitcast(U8))
